import numpy as np
import ml_dtypes


def mxq(x, axis, fmt="e4m3"):
    dtype, down = {"e4m3": (ml_dtypes.float8_e4m3fn, 7), "e5m2": (ml_dtypes.float8_e5m2, 14)}[fmt]
    v = np.moveaxis(np.asarray(x, np.float32).astype(ml_dtypes.bfloat16).astype(np.float64), axis, -1)
    blocks = v.reshape(v.shape[:-1] + (-1, 32))
    amax = np.abs(blocks).max(-1, keepdims=True)
    byte = np.maximum(np.where(amax > 0, np.frexp(amax)[1] - 1 + 127, 0) - down, 1)
    scale = np.exp2(byte - 127.0)
    codes = (blocks / scale).astype(np.float32).astype(dtype).astype(np.float64)
    return np.moveaxis((codes * scale).reshape(v.shape), -1, axis)


WIDE = False


def mx_kscale(k):
    if not WIDE:
        return np.ones(k)
    levels = np.array([10, -10, 5, -5, 0])
    a = np.random.permutation(np.resize(levels, k // 512 * 4)).reshape(k // 512, 4)
    idx = np.arange(k)
    return np.exp2(a[idx // 512, idx % 128 // 32])


BF16 = ml_dtypes.bfloat16


def bf(x):
    return np.asarray(x, np.float32).astype(BF16)


def f64(x):
    return np.asarray(x).astype(np.float64)


B, S, H, DK, F = 1, 128, 8, 64, 1024
D = H * DK
EPS = 1e-14


def layer_norm(u, gamma, beta):
    mean = u.mean(-1, keepdims=True)
    var = np.square(u - mean).mean(-1, keepdims=True)
    return (u - mean) / np.sqrt(var + EPS) * gamma + beta


def setup_inputs():
    r = np.random.standard_normal
    t = mx_kscale(F)
    return {"h": bf(r((B, S, D))),
            "W1": bf(r((D, F)) / np.sqrt(D) * t),
            "b1": bf(0.3 * r(F) * t),
            "W2": bf(r((F, D)) / np.sqrt(F) / t[:, None]),
            "b2": bf(0.3 * r(D)),
            "gamma2": bf(1.0 + 0.1 * r(D)),
            "beta2": bf(0.1 * r(D))}


def reference(h, W1, b1, W2, b2, gamma2, beta2):
    hh = f64(h)
    f = (mxq(hh, 2, "e4m3") @ mxq(f64(W1), 0, "e4m3")) + f64(b1)
    f = (mxq(f, 2, "e4m3") @ mxq(f64(W2), 0, "e4m3")) + f64(b2)
    return layer_norm(hh + f, f64(gamma2), f64(beta2))

@@ -1,0 +1,248 @@
+from contextlib import ExitStack
+
+import concourse.mybir as mybir
+from concourse.masks import make_identity
+
+F32 = mybir.dt.float32
+BF16 = mybir.dt.bfloat16
+U32 = mybir.dt.uint32
+U8 = mybir.dt.uint8
+FP8X4 = mybir.dt.float8_e4m3fn_x4
+ALU = mybir.AluOpType
+ACT = mybir.ActivationFunctionType
+
+P = 128
+PACK = 4
+K_PASS = P * PACK
+
+TOKENS = 128
+D_MODEL = 512
+D_HIDDEN = 1024
+EPS = 1e-14
+PASSES_2 = D_HIDDEN // K_PASS
+
+LOAD_COLS = 512
+PIECE = 256
+RUN = 4
+SCALAR_COLS = PIECE * 5 // 8
+
+FLOPS = 2 * TOKENS * D_MODEL * D_HIDDEN * 2
+
+
+def regroup(nc, grouped, raw):
+    for copy, cols in (
+        (nc.scalar.copy, slice(0, SCALAR_COLS)),
+        (nc.vector.tensor_copy, slice(SCALAR_COLS, PIECE)),
+    ):
+        copy(
+            out=grouped[:, cols, :].rearrange("p (c i) j -> p c j i", i=RUN),
+            in_=raw[:, :, cols].rearrange("p j (c i) -> p c j i", i=RUN),
+        )
+
+
+def quantise(nc, codes, scales, grouped):
+    nc.vector.quantize_mx(
+        out=codes.bitcast(FP8X4),
+        scales=scales,
+        in_=grouped.rearrange("p c j -> p (c j)"),
+    )
+
+
+def tile_encoderblock_pb_s_kernel(tc, h, W1, b1, W2, b2, gamma2, beta2, out):
+    nc = tc.nc
+    with ExitStack() as ctx:
+        keep = ctx.enter_context(tc.tile_pool(name="keep", bufs=1))
+        psum = ctx.enter_context(tc.psum_pool(name="psum", bufs=1))
+
+        vec_rows = keep.tile([P, P], BF16)
+        nc.vector.memset(vec_rows[:], 0.0)
+        eps = keep.tile([P, 1], F32)
+        nc.vector.memset(eps[:], EPS)
+        ident_f32 = keep.tile([P, P], F32)
+        make_identity(nc, ident_f32[:])
+        ident_bf16 = keep.tile([P, P], BF16)
+        make_identity(nc, ident_bf16[:])
+
+        h_sb = keep.tile([TOKENS, D_MODEL], BF16)
+        nc.scalar.dma_start(out=h_sb[:], in_=h.rearrange("b s d -> (b s) d"))
+        B1_ROW, B2_ROW, GAMMA_ROW, BETA_ROW, ROWS_END = 0, 8, 12, 16, 20
+        for vector, row, row_end in (
+            (b1, B1_ROW, B2_ROW),
+            (b2, B2_ROW, GAMMA_ROW),
+            (gamma2, GAMMA_ROW, BETA_ROW),
+            (beta2, BETA_ROW, ROWS_END),
+        ):
+            nc.scalar.dma_start(
+                out=vec_rows[row:row_end, :], in_=vector.rearrange("(c p) -> c p", p=P)
+            )
+
+        table_warm = keep.tile([P, 1], F32)
+        nc.scalar.activation(out=table_warm[:], in_=eps[:], func=ACT.Sqrt)
+
+        w1_raw = keep.tile([P, PACK, D_HIDDEN], BF16)
+        w1_rows = W1.rearrange("(p j) f -> p j f", j=PACK)
+        for c in range(0, D_HIDDEN, LOAD_COLS):
+            nc.sync.dma_start(
+                out=w1_raw[:, :, c : c + LOAD_COLS], in_=w1_rows[:, :, c : c + LOAD_COLS]
+            )
+        w2_raw = keep.tile([P, PASSES_2, PACK, D_MODEL], BF16)
+        w2_rows = W2.rearrange("(g j p) n -> g p j n", j=PACK, p=P)
+        for g in range(PASSES_2):
+            nc.sync.dma_start(out=w2_raw[:, g, :, :], in_=w2_rows[g])
+
+        h_words = h_sb[:].bitcast(F32).rearrange("r (p u) -> r u p", u=2)
+        hT_ps = psum.tile([P, 2, TOKENS], F32)
+        for u in range(2):
+            nc.tensor.transpose(hT_ps[:, u, :], h_words[:, u, :], ident_f32[:])
+        h_grouped = keep.tile([P, TOKENS * PACK], BF16, align_bytes=64)
+        nc.scalar.copy(
+            out=h_grouped[:].bitcast(F32).rearrange("p (r u) -> p r u", u=2),
+            in_=hT_ps[:].rearrange("p u r -> p r u"),
+        )
+        h_codes = keep.tile([P, TOKENS], U32, align_bytes=64)
+        h_scales = keep.tile([P, TOKENS], U8, align_bytes=64)
+        nc.vector.quantize_mx(
+            out=h_codes[:].bitcast(FP8X4), scales=h_scales[:], in_=h_grouped[:]
+        )
+
+        vec_ps = psum.tile([P, P], BF16)
+        nc.tensor.transpose(vec_ps[:], vec_rows[:], ident_bf16[:])
+        vec_cols = keep.tile([P, ROWS_END], BF16)
+        nc.vector.tensor_copy(out=vec_cols[:], in_=vec_ps[:, 0:ROWS_END])
+
+        b2_ps = psum.tile([P, D_MODEL], BF16)
+        affine_ps = psum.tile([P, 2, D_MODEL], BF16)
+        for row, spread in (
+            (B2_ROW, b2_ps[:]),
+            (GAMMA_ROW, affine_ps[:, 0, :]),
+            (BETA_ROW, affine_ps[:, 1, :]),
+        ):
+            for c in range(D_MODEL // P):
+                nc.tensor.transpose(
+                    spread[:, c * P : (c + 1) * P],
+                    vec_cols[:, row + c : row + c + 1].to_broadcast([P, P]),
+                    ident_bf16[:],
+                )
+        h_plus_b2 = keep.tile([TOKENS, D_MODEL], F32)
+        nc.vector.tensor_tensor(out=h_plus_b2[:], in0=h_sb[:], in1=b2_ps[:], op=ALU.add)
+
+        w1_grouped = keep.tile([P, D_HIDDEN, PACK], BF16, align_bytes=64)
+        w1_codes = keep.tile([P, D_HIDDEN], U32, align_bytes=64)
+        w1_scales = keep.tile([P, D_HIDDEN], U8, align_bytes=64)
+        w2_grouped = keep.tile([P, PASSES_2, D_MODEL, PACK], BF16, align_bytes=64)
+        w2_codes = keep.tile([P, PASSES_2, D_MODEL], U32, align_bytes=64)
+        w2_scales = keep.tile([P, PASSES_2, D_MODEL], U8, align_bytes=64)
+        f1_grouped = keep.tile([P, PASSES_2, TOKENS, PACK], BF16, align_bytes=64)
+        f1_codes = keep.tile([P, PASSES_2, TOKENS], U32, align_bytes=64)
+        f1_scales = keep.tile([P, PASSES_2, TOKENS], U8, align_bytes=64)
+
+        f1_ps = [psum.tile([P, PACK, TOKENS], F32, name="f1_ps%d" % g) for g in range(PASSES_2)]
+        HALVES = D_MODEL // PIECE
+        f2_ps = [psum.tile([TOKENS, PIECE], F32, name="f2_ps%d" % n) for n in range(HALVES)]
+
+        pieces = []
+        for c in range(0, D_HIDDEN, PIECE):
+            cols = slice(c, c + PIECE)
+            pieces.append(
+                (w1_raw[:, :, cols], w1_grouped[:, cols, :], w1_codes[:, cols], w1_scales[:, cols])
+            )
+        W1_PIECES = len(pieces)
+        for g in range(PASSES_2):
+            for c in range(0, D_MODEL, PIECE):
+                cols = slice(c, c + PIECE)
+                pieces.append(
+                    (
+                        w2_raw[:, g, :, cols],
+                        w2_grouped[:, g, cols, :],
+                        w2_codes[:, g, cols],
+                        w2_scales[:, g, cols],
+                    )
+                )
+
+        def first_layer(piece):
+            for unit0 in range(piece * PIECE, (piece + 1) * PIECE, P):
+                g, j = divmod(unit0 // P, PACK)
+                nc.tensor.matmul_mx(
+                    out=f1_ps[g][:, j, :],
+                    lhsT=w1_codes[:, unit0 : unit0 + P].bitcast(FP8X4),
+                    lhsT_scale=w1_scales[:, unit0 : unit0 + P],
+                    rhs=h_codes[:].bitcast(FP8X4),
+                    rhs_scale=h_scales[:],
+                    start=True,
+                    stop=True,
+                )
+
+        def hidden_to_mx(g):
+            nc.vector.tensor_tensor(
+                out=f1_grouped[:, g, :, :],
+                in0=f1_ps[g][:].rearrange("p j r -> p r j"),
+                in1=vec_cols[:, B1_ROW + g * PACK : B1_ROW + (g + 1) * PACK]
+                .unsqueeze(1)
+                .to_broadcast([P, TOKENS, PACK]),
+                op=ALU.add,
+            )
+            quantise(nc, f1_codes[:, g, :], f1_scales[:, g, :], f1_grouped[:, g, :, :])
+
+        def second_layer(g, n):
+            cols = slice(n * PIECE, (n + 1) * PIECE)
+            nc.tensor.matmul_mx(
+                out=f2_ps[n][:],
+                lhsT=f1_codes[:, g, :].bitcast(FP8X4),
+                lhsT_scale=f1_scales[:, g, :],
+                rhs=w2_codes[:, g, cols].bitcast(FP8X4),
+                rhs_scale=w2_scales[:, g, cols],
+                start=(g == 0),
+                stop=(g == PASSES_2 - 1),
+            )
+
+        PIECES_PER_PASS = K_PASS // PIECE
+        for step in range(len(pieces) + 1):
+            if step < len(pieces):
+                raw, grouped, codes, scales = pieces[step]
+                regroup(nc, grouped, raw)
+            ready = step - 1
+            if ready >= 0:
+                raw, grouped, codes, scales = pieces[ready]
+                quantise(nc, codes, scales, grouped)
+            if 0 <= ready < W1_PIECES:
+                first_layer(ready)
+            if ready >= W1_PIECES:
+                g, n = divmod(ready - W1_PIECES, HALVES)
+                second_layer(g, n)
+            multiplied = step - 2
+            if 0 <= multiplied < W1_PIECES and (multiplied + 1) % PIECES_PER_PASS == 0:
+                hidden_to_mx(multiplied // PIECES_PER_PASS)
+
+        u = keep.tile([TOKENS, D_MODEL], F32)
+        stats = keep.tile([TOKENS, HALVES, 6], F32)
+        for n in range(HALVES):
+            cols = slice(n * PIECE, (n + 1) * PIECE)
+            nc.vector.tensor_tensor(
+                out=u[:, cols], in0=f2_ps[n][:], in1=h_plus_b2[:, cols], op=ALU.add
+            )
+            nc.vector.bn_stats(out=stats[:, n, :], in_=u[:, cols])
+        mean_var = keep.tile([TOKENS, 2], F32)
+        nc.vector.bn_aggr(out=mean_var[:], in_=stats[:].rearrange("p n s -> p (n s)"))
+        std = keep.tile([TOKENS, 1], F32)
+        nc.scalar.activation(out=std[:], in_=mean_var[:, 1:2], func=ACT.Sqrt, bias=eps[:])
+        centred = keep.tile([TOKENS, D_MODEL], F32)
+        nc.vector.scalar_tensor_tensor(
+            out=centred[:],
+            in0=u[:],
+            scalar=mean_var[:, 0:1],
+            in1=affine_ps[:, 0, :],
+            op0=ALU.subtract,
+            op1=ALU.mult,
+        )
+        rstd = keep.tile([TOKENS, 1], F32)
+        nc.vector.reciprocal(out=rstd[:], in_=std[:])
+        result = keep.tile([TOKENS, D_MODEL], F32)
+        nc.vector.scalar_tensor_tensor(
+            out=result[:],
+            in0=centred[:],
+            scalar=rstd[:],
+            in1=affine_ps[:, 1, :],
+            op0=ALU.mult,
+            op1=ALU.add,
+        )
+        nc.sync.dma_start(out=out.rearrange("b s d -> (b s) d"), in_=result[:])

@@ -53,6 +53,7 @@ def tile_encoderblock_pb_s_kernel(tc, h, W1, b1, W2, b2, gamma2, beta2, out):
     with ExitStack() as ctx:
         keep = ctx.enter_context(tc.tile_pool(name="keep", bufs=1))
         psum = ctx.enter_context(tc.psum_pool(name="psum", bufs=1))
+        ctx.enter_context(tc.manual_schedule())
 
         vec_rows = keep.tile([P, P], BF16)
         nc.vector.memset(vec_rows[:], 0.0)
@@ -79,16 +80,16 @@ def tile_encoderblock_pb_s_kernel(tc, h, W1, b1, W2, b2, gamma2, beta2, out):
         table_warm = keep.tile([P, 1], F32)
         nc.scalar.activation(out=table_warm[:], in_=eps[:], func=ACT.Sqrt)
 
-        w1_raw = keep.tile([P, PACK, D_HIDDEN], BF16)
         w1_rows = W1.rearrange("(p j) f -> p j f", j=PACK)
-        for c in range(0, D_HIDDEN, LOAD_COLS):
-            nc.sync.dma_start(
-                out=w1_raw[:, :, c : c + LOAD_COLS], in_=w1_rows[:, :, c : c + LOAD_COLS]
-            )
-        w2_raw = keep.tile([P, PASSES_2, PACK, D_MODEL], BF16)
         w2_rows = W2.rearrange("(g j p) n -> g p j n", j=PACK, p=P)
-        for g in range(PASSES_2):
-            nc.sync.dma_start(out=w2_raw[:, g, :, :], in_=w2_rows[g])
+        sources = [w1_rows[:, :, c : c + LOAD_COLS] for c in range(0, D_HIDDEN, LOAD_COLS)]
+        W1_LOADS = len(sources)
+        sources.extend([w2_rows[g] for g in range(PASSES_2)])
+        raws = []
+        for i, source in enumerate(sources):
+            raw = keep.tile([P, PACK, LOAD_COLS], BF16, name="raw%d" % i)
+            nc.sync.dma_start(out=raw[:], in_=source)
+            raws.append(raw)
 
         h_words = h_sb[:].bitcast(F32).rearrange("r (p u) -> r u p", u=2)
         hT_ps = psum.tile([P, 2, TOKENS], F32)
@@ -106,116 +107,134 @@ def tile_encoderblock_pb_s_kernel(tc, h, W1, b1, W2, b2, gamma2, beta2, out):
         )
 
         vec_ps = psum.tile([P, P], BF16)
-        nc.tensor.transpose(vec_ps[:], vec_rows[:], ident_bf16[:])
         vec_cols = keep.tile([P, ROWS_END], BF16)
-        nc.vector.tensor_copy(out=vec_cols[:], in_=vec_ps[:, 0:ROWS_END])
-
         b2_ps = psum.tile([P, D_MODEL], BF16)
         affine_ps = psum.tile([P, 2, D_MODEL], BF16)
-        for row, spread in (
-            (B2_ROW, b2_ps[:]),
-            (GAMMA_ROW, affine_ps[:, 0, :]),
-            (BETA_ROW, affine_ps[:, 1, :]),
-        ):
-            for c in range(D_MODEL // P):
-                nc.tensor.transpose(
-                    spread[:, c * P : (c + 1) * P],
-                    vec_cols[:, row + c : row + c + 1].to_broadcast([P, P]),
-                    ident_bf16[:],
-                )
         h_plus_b2 = keep.tile([TOKENS, D_MODEL], F32)
-        nc.vector.tensor_tensor(out=h_plus_b2[:], in0=h_sb[:], in1=b2_ps[:], op=ALU.add)
 
-        w1_grouped = keep.tile([P, D_HIDDEN, PACK], BF16, align_bytes=64)
-        w1_codes = keep.tile([P, D_HIDDEN], U32, align_bytes=64)
-        w1_scales = keep.tile([P, D_HIDDEN], U8, align_bytes=64)
-        w2_grouped = keep.tile([P, PASSES_2, D_MODEL, PACK], BF16, align_bytes=64)
-        w2_codes = keep.tile([P, PASSES_2, D_MODEL], U32, align_bytes=64)
-        w2_scales = keep.tile([P, PASSES_2, D_MODEL], U8, align_bytes=64)
-        f1_grouped = keep.tile([P, PASSES_2, TOKENS, PACK], BF16, align_bytes=64)
-        f1_codes = keep.tile([P, PASSES_2, TOKENS], U32, align_bytes=64)
-        f1_scales = keep.tile([P, PASSES_2, TOKENS], U8, align_bytes=64)
+        def stand_vectors_up():
+            nc.tensor.transpose(vec_ps[:], vec_rows[:], ident_bf16[:])
 
-        f1_ps = [psum.tile([P, PACK, TOKENS], F32, name="f1_ps%d" % g) for g in range(PASSES_2)]
-        HALVES = D_MODEL // PIECE
-        f2_ps = [psum.tile([TOKENS, PIECE], F32, name="f2_ps%d" % n) for n in range(HALVES)]
-
-        pieces = []
-        for c in range(0, D_HIDDEN, PIECE):
-            cols = slice(c, c + PIECE)
-            pieces.append(
-                (w1_raw[:, :, cols], w1_grouped[:, cols, :], w1_codes[:, cols], w1_scales[:, cols])
-            )
-        W1_PIECES = len(pieces)
-        for g in range(PASSES_2):
-            for c in range(0, D_MODEL, PIECE):
-                cols = slice(c, c + PIECE)
-                pieces.append(
-                    (
-                        w2_raw[:, g, :, cols],
-                        w2_grouped[:, g, cols, :],
-                        w2_codes[:, g, cols],
-                        w2_scales[:, g, cols],
+        def spread_vectors():
+            nc.scalar.copy(out=vec_cols[:], in_=vec_ps[:, 0:ROWS_END])
+            for row, spread in (
+                (B2_ROW, b2_ps[:]),
+                (GAMMA_ROW, affine_ps[:, 0, :]),
+                (BETA_ROW, affine_ps[:, 1, :]),
+            ):
+                for c in range(D_MODEL // P):
+                    nc.tensor.transpose(
+                        spread[:, c * P : (c + 1) * P],
+                        vec_cols[:, row + c : row + c + 1].to_broadcast([P, P]),
+                        ident_bf16[:],
                     )
-                )
 
-        def first_layer(piece):
-            for unit0 in range(piece * PIECE, (piece + 1) * PIECE, P):
-                g, j = divmod(unit0 // P, PACK)
+        def add_b2_to_h():
+            nc.vector.tensor_tensor(out=h_plus_b2[:], in0=h_sb[:], in1=b2_ps[:], op=ALU.add)
+
+        PIECES_PER_LOAD = LOAD_COLS // PIECE
+        N_PIECES = len(raws) * PIECES_PER_LOAD
+        W1_PIECES = W1_LOADS * PIECES_PER_LOAD
+        grouped = [
+            keep.tile([P, PIECE, PACK], BF16, align_bytes=64, name="grouped%d" % i)
+            for i in range(N_PIECES)
+        ]
+        codes = [
+            keep.tile([P, PIECE], U32, align_bytes=64, name="codes%d" % i)
+            for i in range(N_PIECES)
+        ]
+        scales = [
+            keep.tile([P, PIECE], U8, align_bytes=64, name="scales%d" % i)
+            for i in range(N_PIECES)
+        ]
+        f1_grouped = [
+            keep.tile([P, TOKENS, PACK], BF16, align_bytes=64, name="f1_grouped%d" % g)
+            for g in range(PASSES_2)
+        ]
+        f1_codes = [
+            keep.tile([P, TOKENS], U32, align_bytes=64, name="f1_codes%d" % g)
+            for g in range(PASSES_2)
+        ]
+        f1_scales = [
+            keep.tile([P, TOKENS], U8, align_bytes=64, name="f1_scales%d" % g)
+            for g in range(PASSES_2)
+        ]
+        f1_ps = [psum.tile([P, PACK, TOKENS], F32, name="f1_ps%d" % g) for g in range(PASSES_2)]
+        f2_ps = [
+            psum.tile([TOKENS, PIECE], F32, name="f2_ps%d" % n) for n in range(PIECES_PER_LOAD)
+        ]
+
+        def regroup_piece(i):
+            load, part = divmod(i, PIECES_PER_LOAD)
+            regroup(nc, grouped[i][:], raws[load][:, :, part * PIECE : (part + 1) * PIECE])
+
+        def first_layer(i):
+            for m in range(0, PIECE, P):
+                g, j = divmod((i * PIECE + m) // P, PACK)
                 nc.tensor.matmul_mx(
                     out=f1_ps[g][:, j, :],
-                    lhsT=w1_codes[:, unit0 : unit0 + P].bitcast(FP8X4),
-                    lhsT_scale=w1_scales[:, unit0 : unit0 + P],
+                    lhsT=codes[i][:, m : m + P].bitcast(FP8X4),
+                    lhsT_scale=scales[i][:, m : m + P],
                     rhs=h_codes[:].bitcast(FP8X4),
                     rhs_scale=h_scales[:],
                     start=True,
                     stop=True,
                 )
 
-        def hidden_to_mx(g):
+        def add_b1(g):
             nc.vector.tensor_tensor(
-                out=f1_grouped[:, g, :, :],
+                out=f1_grouped[g][:],
                 in0=f1_ps[g][:].rearrange("p j r -> p r j"),
                 in1=vec_cols[:, B1_ROW + g * PACK : B1_ROW + (g + 1) * PACK]
                 .unsqueeze(1)
                 .to_broadcast([P, TOKENS, PACK]),
                 op=ALU.add,
             )
-            quantise(nc, f1_codes[:, g, :], f1_scales[:, g, :], f1_grouped[:, g, :, :])
 
-        def second_layer(g, n):
-            cols = slice(n * PIECE, (n + 1) * PIECE)
+        def second_layer(i):
+            g, n = divmod(i - W1_PIECES, PIECES_PER_LOAD)
             nc.tensor.matmul_mx(
                 out=f2_ps[n][:],
-                lhsT=f1_codes[:, g, :].bitcast(FP8X4),
-                lhsT_scale=f1_scales[:, g, :],
-                rhs=w2_codes[:, g, cols].bitcast(FP8X4),
-                rhs_scale=w2_scales[:, g, cols],
+                lhsT=f1_codes[g][:].bitcast(FP8X4),
+                lhsT_scale=f1_scales[g][:],
+                rhs=codes[i][:].bitcast(FP8X4),
+                rhs_scale=scales[i][:],
                 start=(g == 0),
                 stop=(g == PASSES_2 - 1),
             )
 
-        PIECES_PER_PASS = K_PASS // PIECE
-        for step in range(len(pieces) + 1):
-            if step < len(pieces):
-                raw, grouped, codes, scales = pieces[step]
-                regroup(nc, grouped, raw)
-            ready = step - 1
-            if ready >= 0:
-                raw, grouped, codes, scales = pieces[ready]
-                quantise(nc, codes, scales, grouped)
-            if 0 <= ready < W1_PIECES:
-                first_layer(ready)
-            if ready >= W1_PIECES:
-                g, n = divmod(ready - W1_PIECES, HALVES)
-                second_layer(g, n)
-            multiplied = step - 2
-            if 0 <= multiplied < W1_PIECES and (multiplied + 1) % PIECES_PER_PASS == 0:
-                hidden_to_mx(multiplied // PIECES_PER_PASS)
+        def quantise_f1(g):
+            quantise(nc, f1_codes[g][:], f1_scales[g][:], f1_grouped[g][:])
+
+        def weights_round(i):
+            if i + 1 < N_PIECES:
+                regroup_piece(i + 1)
+            quantise(nc, codes[i][:], scales[i][:], grouped[i][:])
+            if i < W1_PIECES:
+                first_layer(i)
+            else:
+                second_layer(i)
+
+        regroup_piece(0)
+        weights_round(0)
+        stand_vectors_up()
+        weights_round(1)
+        spread_vectors()
+        weights_round(2)
+        add_b1(0)
+        weights_round(3)
+        quantise_f1(0)
+        add_b2_to_h()
+        weights_round(4)
+        add_b1(1)
+        weights_round(5)
+        quantise_f1(1)
+        weights_round(6)
+        weights_round(7)
 
         u = keep.tile([TOKENS, D_MODEL], F32)
-        stats = keep.tile([TOKENS, HALVES, 6], F32)
-        for n in range(HALVES):
+        stats = keep.tile([TOKENS, PIECES_PER_LOAD, 6], F32)
+        for n in range(PIECES_PER_LOAD):
             cols = slice(n * PIECE, (n + 1) * PIECE)
             nc.vector.tensor_tensor(
                 out=u[:, cols], in0=f2_ps[n][:], in1=h_plus_b2[:, cols], op=ALU.add

@@ -78,7 +78,7 @@ def tile_encoderblock_pb_s_kernel(tc, h, W1, b1, W2, b2, gamma2, beta2, out):
             )
 
         table_warm = keep.tile([P, 1], F32)
-        nc.scalar.activation(out=table_warm[:], in_=eps[:], func=ACT.Sqrt)
+        nc.scalar.activation(out=table_warm[:], in_=eps[:], func=ACT.Abs_reciprocal_sqrt)
 
         w1_rows = W1.rearrange("(p j) f -> p j f", j=PACK)
         w2_rows = W2.rearrange("(g j p) n -> g p j n", j=PACK, p=P)
@@ -242,26 +242,30 @@ def tile_encoderblock_pb_s_kernel(tc, h, W1, b1, W2, b2, gamma2, beta2, out):
             nc.vector.bn_stats(out=stats[:, n, :], in_=u[:, cols])
         mean_var = keep.tile([TOKENS, 2], F32)
         nc.vector.bn_aggr(out=mean_var[:], in_=stats[:].rearrange("p n s -> p (n s)"))
-        std = keep.tile([TOKENS, 1], F32)
-        nc.scalar.activation(out=std[:], in_=mean_var[:, 1:2], func=ACT.Sqrt, bias=eps[:])
-        centred = keep.tile([TOKENS, D_MODEL], F32)
-        nc.vector.scalar_tensor_tensor(
-            out=centred[:],
-            in0=u[:],
-            scalar=mean_var[:, 0:1],
-            in1=affine_ps[:, 0, :],
-            op0=ALU.subtract,
-            op1=ALU.mult,
-        )
         rstd = keep.tile([TOKENS, 1], F32)
-        nc.vector.reciprocal(out=rstd[:], in_=std[:])
-        result = keep.tile([TOKENS, D_MODEL], F32)
-        nc.vector.scalar_tensor_tensor(
-            out=result[:],
-            in0=centred[:],
-            scalar=rstd[:],
-            in1=affine_ps[:, 1, :],
-            op0=ALU.mult,
-            op1=ALU.add,
+        nc.scalar.activation(
+            out=rstd[:], in_=mean_var[:, 1:2], func=ACT.Abs_reciprocal_sqrt, bias=eps[:]
         )
-        nc.sync.dma_start(out=out.rearrange("b s d -> (b s) d"), in_=result[:])
+        centred = keep.tile([TOKENS, D_MODEL], F32)
+        halves = [slice(n * PIECE, (n + 1) * PIECE) for n in range(PIECES_PER_LOAD)]
+        for cols in halves:
+            nc.vector.scalar_tensor_tensor(
+                out=centred[:, cols],
+                in0=u[:, cols],
+                scalar=mean_var[:, 0:1],
+                in1=affine_ps[:, 0, cols],
+                op0=ALU.subtract,
+                op1=ALU.mult,
+            )
+        result = keep.tile([TOKENS, D_MODEL], F32)
+        out_rows = out.rearrange("b s d -> (b s) d")
+        for cols in halves:
+            nc.vector.scalar_tensor_tensor(
+                out=result[:, cols],
+                in0=centred[:, cols],
+                scalar=rstd[:],
+                in1=affine_ps[:, 1, cols],
+                op0=ALU.mult,
+                op1=ALU.add,
+            )
+            nc.sync.dma_start(out=out_rows[:, cols], in_=result[:, cols])

@@ -93,18 +93,22 @@ def tile_encoderblock_pb_s_kernel(tc, h, W1, b1, W2, b2, gamma2, beta2, out):
 
         h_words = h_sb[:].bitcast(F32).rearrange("r (p u) -> r u p", u=2)
         hT_ps = psum.tile([P, 2, TOKENS], F32)
-        for u in range(2):
-            nc.tensor.transpose(hT_ps[:, u, :], h_words[:, u, :], ident_f32[:])
         h_grouped = keep.tile([P, TOKENS * PACK], BF16, align_bytes=64)
-        nc.scalar.copy(
-            out=h_grouped[:].bitcast(F32).rearrange("p (r u) -> p r u", u=2),
-            in_=hT_ps[:].rearrange("p u r -> p r u"),
-        )
         h_codes = keep.tile([P, TOKENS], U32, align_bytes=64)
         h_scales = keep.tile([P, TOKENS], U8, align_bytes=64)
-        nc.vector.quantize_mx(
-            out=h_codes[:].bitcast(FP8X4), scales=h_scales[:], in_=h_grouped[:]
-        )
+
+        def stand_h_up():
+            for u in range(2):
+                nc.tensor.transpose(hT_ps[:, u, :], h_words[:, u, :], ident_f32[:])
+            nc.scalar.copy(
+                out=h_grouped[:].bitcast(F32).rearrange("p (r u) -> p r u", u=2),
+                in_=hT_ps[:].rearrange("p u r -> p r u"),
+            )
+
+        def quantise_h():
+            nc.vector.quantize_mx(
+                out=h_codes[:].bitcast(FP8X4), scales=h_scales[:], in_=h_grouped[:]
+            )
 
         vec_ps = psum.tile([P, P], BF16)
         vec_cols = keep.tile([P, ROWS_END], BF16)
@@ -206,17 +210,24 @@ def tile_encoderblock_pb_s_kernel(tc, h, W1, b1, W2, b2, gamma2, beta2, out):
         def quantise_f1(g):
             quantise(nc, f1_codes[g][:], f1_scales[g][:], f1_grouped[g][:])
 
+        def quantise_piece(i):
+            quantise(nc, codes[i][:], scales[i][:], grouped[i][:])
+
+        def multiply(i):
+            (first_layer if i < W1_PIECES else second_layer)(i)
+
         def weights_round(i):
             if i + 1 < N_PIECES:
                 regroup_piece(i + 1)
-            quantise(nc, codes[i][:], scales[i][:], grouped[i][:])
-            if i < W1_PIECES:
-                first_layer(i)
-            else:
-                second_layer(i)
+            quantise_piece(i)
+            multiply(i)
 
         regroup_piece(0)
-        weights_round(0)
+        regroup_piece(1)
+        stand_h_up()
+        quantise_piece(0)
+        quantise_h()
+        multiply(0)
         stand_vectors_up()
         weights_round(1)
         spread_vectors()

@@ -21,8 +21,9 @@ D_HIDDEN = 1024
 EPS = 1e-14
 PASSES_2 = D_HIDDEN // K_PASS
 
-LOAD_COLS = 512
 PIECE = 256
+W1_LOADS = (256, 256, 512)
+W2_LOADS = (512,)
 RUN = 4
 SCALAR_COLS = PIECE * 5 // 8
 
@@ -82,14 +83,18 @@ def tile_encoderblock_pb_s_kernel(tc, h, W1, b1, W2, b2, gamma2, beta2, out):
 
         w1_rows = W1.rearrange("(p j) f -> p j f", j=PACK)
         w2_rows = W2.rearrange("(g j p) n -> g p j n", j=PACK, p=P)
-        sources = [w1_rows[:, :, c : c + LOAD_COLS] for c in range(0, D_HIDDEN, LOAD_COLS)]
-        W1_LOADS = len(sources)
-        sources.extend([w2_rows[g] for g in range(PASSES_2)])
-        raws = []
-        for i, source in enumerate(sources):
-            raw = keep.tile([P, PACK, LOAD_COLS], BF16, name="raw%d" % i)
+        loads = []
+        for rows, widths in ((w1_rows, W1_LOADS), (w2_rows[0], W2_LOADS), (w2_rows[1], W2_LOADS)):
+            start = 0
+            for width in widths:
+                loads.append(rows[:, :, start : start + width])
+                start += width
+        raw_pieces = []
+        for i, source in enumerate(loads):
+            width = source.shape[2]
+            raw = keep.tile([P, PACK, width], BF16, name="raw%d" % i)
             nc.sync.dma_start(out=raw[:], in_=source)
-            raws.append(raw)
+            raw_pieces.extend([raw[:, :, c : c + PIECE] for c in range(0, width, PIECE)])
 
         h_words = h_sb[:].bitcast(F32).rearrange("r (p u) -> r u p", u=2)
         hT_ps = psum.tile([P, 2, TOKENS], F32)
@@ -136,9 +141,9 @@ def tile_encoderblock_pb_s_kernel(tc, h, W1, b1, W2, b2, gamma2, beta2, out):
         def add_b2_to_h():
             nc.vector.tensor_tensor(out=h_plus_b2[:], in0=h_sb[:], in1=b2_ps[:], op=ALU.add)
 
-        PIECES_PER_LOAD = LOAD_COLS // PIECE
-        N_PIECES = len(raws) * PIECES_PER_LOAD
-        W1_PIECES = W1_LOADS * PIECES_PER_LOAD
+        N_PIECES = len(raw_pieces)
+        W1_PIECES = D_HIDDEN // PIECE
+        OUT_PIECES = D_MODEL // PIECE
         grouped = [
             keep.tile([P, PIECE, PACK], BF16, align_bytes=64, name="grouped%d" % i)
             for i in range(N_PIECES)
@@ -165,12 +170,11 @@ def tile_encoderblock_pb_s_kernel(tc, h, W1, b1, W2, b2, gamma2, beta2, out):
         ]
         f1_ps = [psum.tile([P, PACK, TOKENS], F32, name="f1_ps%d" % g) for g in range(PASSES_2)]
         f2_ps = [
-            psum.tile([TOKENS, PIECE], F32, name="f2_ps%d" % n) for n in range(PIECES_PER_LOAD)
+            psum.tile([TOKENS, PIECE], F32, name="f2_ps%d" % n) for n in range(OUT_PIECES)
         ]
 
         def regroup_piece(i):
-            load, part = divmod(i, PIECES_PER_LOAD)
-            regroup(nc, grouped[i][:], raws[load][:, :, part * PIECE : (part + 1) * PIECE])
+            regroup(nc, grouped[i][:], raw_pieces[i])
 
         def first_layer(i):
             for m in range(0, PIECE, P):
@@ -196,7 +200,7 @@ def tile_encoderblock_pb_s_kernel(tc, h, W1, b1, W2, b2, gamma2, beta2, out):
             )
 
         def second_layer(i):
-            g, n = divmod(i - W1_PIECES, PIECES_PER_LOAD)
+            g, n = divmod(i - W1_PIECES, OUT_PIECES)
             nc.tensor.matmul_mx(
                 out=f2_ps[n][:],
                 lhsT=f1_codes[g][:].bitcast(FP8X4),
@@ -244,8 +248,8 @@ def tile_encoderblock_pb_s_kernel(tc, h, W1, b1, W2, b2, gamma2, beta2, out):
         weights_round(7)
 
         u = keep.tile([TOKENS, D_MODEL], F32)
-        stats = keep.tile([TOKENS, PIECES_PER_LOAD, 6], F32)
-        for n in range(PIECES_PER_LOAD):
+        stats = keep.tile([TOKENS, OUT_PIECES, 6], F32)
+        for n in range(OUT_PIECES):
             cols = slice(n * PIECE, (n + 1) * PIECE)
             nc.vector.tensor_tensor(
                 out=u[:, cols], in0=f2_ps[n][:], in1=h_plus_b2[:, cols], op=ALU.add
@@ -258,7 +262,7 @@ def tile_encoderblock_pb_s_kernel(tc, h, W1, b1, W2, b2, gamma2, beta2, out):
             out=rstd[:], in_=mean_var[:, 1:2], func=ACT.Abs_reciprocal_sqrt, bias=eps[:]
         )
         centred = keep.tile([TOKENS, D_MODEL], F32)
-        halves = [slice(n * PIECE, (n + 1) * PIECE) for n in range(PIECES_PER_LOAD)]
+        halves = [slice(n * PIECE, (n + 1) * PIECE) for n in range(OUT_PIECES)]
         for cols in halves:
             nc.vector.scalar_tensor_tensor(
                 out=centred[:, cols],

@@ -25,7 +25,7 @@ PIECE = 256
 W1_LOADS = (256, 256, 512)
 W2_LOADS = (512,)
 RUN = 4
-SCALAR_COLS = PIECE * 5 // 8
+SCALAR_COLS = PIECE * 3 // 4
 
 FLOPS = 2 * TOKENS * D_MODEL * D_HIDDEN * 2
 
@@ -231,8 +231,8 @@ def tile_encoderblock_pb_s_kernel(tc, h, W1, b1, W2, b2, gamma2, beta2, out):
         stand_h_up()
         quantise_piece(0)
         quantise_h()
-        multiply(0)
         stand_vectors_up()
+        multiply(0)
         weights_round(1)
         spread_vectors()
         weights_round(2)
@@ -254,6 +254,8 @@ def tile_encoderblock_pb_s_kernel(tc, h, W1, b1, W2, b2, gamma2, beta2, out):
             nc.vector.tensor_tensor(
                 out=u[:, cols], in0=f2_ps[n][:], in1=h_plus_b2[:, cols], op=ALU.add
             )
+        for n in range(OUT_PIECES):
+            cols = slice(n * PIECE, (n + 1) * PIECE)
             nc.vector.bn_stats(out=stats[:, n, :], in_=u[:, cols])
         mean_var = keep.tile([TOKENS, 2], F32)
         nc.vector.bn_aggr(out=mean_var[:], in_=stats[:].rearrange("p n s -> p (n s)"))

@@ -22,18 +22,20 @@ EPS = 1e-14
 PASSES_2 = D_HIDDEN // K_PASS
 
 PIECE = 256
-W1_LOADS = (256, 256, 512)
+W1_LOADS = (256, 256, 256, 256)
 W2_LOADS = (512,)
 RUN = 4
-SCALAR_COLS = PIECE * 3 // 4
+FIRST_PIECES = 2
+SCALAR_COLS_FIRST = PIECE // 2
+SCALAR_COLS = PIECE * 13 // 16
 
 FLOPS = 2 * TOKENS * D_MODEL * D_HIDDEN * 2
 
 
-def regroup(nc, grouped, raw):
+def regroup(nc, grouped, raw, scalar_cols):
     for copy, cols in (
-        (nc.scalar.copy, slice(0, SCALAR_COLS)),
-        (nc.vector.tensor_copy, slice(SCALAR_COLS, PIECE)),
+        (nc.scalar.copy, slice(0, scalar_cols)),
+        (nc.vector.tensor_copy, slice(scalar_cols, PIECE)),
     ):
         copy(
             out=grouped[:, cols, :].rearrange("p (c i) j -> p c j i", i=RUN),
@@ -56,8 +58,10 @@ def tile_encoderblock_pb_s_kernel(tc, h, W1, b1, W2, b2, gamma2, beta2, out):
         psum = ctx.enter_context(tc.psum_pool(name="psum", bufs=1))
         ctx.enter_context(tc.manual_schedule())
 
-        vec_rows = keep.tile([P, P], BF16)
-        nc.vector.memset(vec_rows[:], 0.0)
+        bias_rows = keep.tile([P, P], BF16)
+        nc.vector.memset(bias_rows[:], 0.0)
+        affine_rows = keep.tile([P, P], BF16)
+        nc.vector.memset(affine_rows[:], 0.0)
         eps = keep.tile([P, 1], F32)
         nc.vector.memset(eps[:], EPS)
         ident_f32 = keep.tile([P, P], F32)
@@ -67,16 +71,12 @@ def tile_encoderblock_pb_s_kernel(tc, h, W1, b1, W2, b2, gamma2, beta2, out):
 
         h_sb = keep.tile([TOKENS, D_MODEL], BF16)
         nc.scalar.dma_start(out=h_sb[:], in_=h.rearrange("b s d -> (b s) d"))
-        B1_ROW, B2_ROW, GAMMA_ROW, BETA_ROW, ROWS_END = 0, 8, 12, 16, 20
-        for vector, row, row_end in (
-            (b1, B1_ROW, B2_ROW),
-            (b2, B2_ROW, GAMMA_ROW),
-            (gamma2, GAMMA_ROW, BETA_ROW),
-            (beta2, BETA_ROW, ROWS_END),
-        ):
-            nc.scalar.dma_start(
-                out=vec_rows[row:row_end, :], in_=vector.rearrange("(c p) -> c p", p=P)
-            )
+        B1_ROW, B2_ROW, BIAS_ROWS = 0, 8, 12
+        GAMMA_ROW, BETA_ROW, AFFINE_ROWS = 0, 4, 8
+        biases = (
+            (bias_rows[B1_ROW:B2_ROW, :], b1.rearrange("(c p) -> c p", p=P)),
+            (bias_rows[B2_ROW:BIAS_ROWS, :], b2.rearrange("(c p) -> c p", p=P)),
+        )
 
         table_warm = keep.tile([P, 1], F32)
         nc.scalar.activation(out=table_warm[:], in_=eps[:], func=ACT.Abs_reciprocal_sqrt)
@@ -94,7 +94,16 @@ def tile_encoderblock_pb_s_kernel(tc, h, W1, b1, W2, b2, gamma2, beta2, out):
             width = source.shape[2]
             raw = keep.tile([P, PACK, width], BF16, name="raw%d" % i)
             nc.sync.dma_start(out=raw[:], in_=source)
+            if i == 0:
+                for rows, vector in biases:
+                    nc.sync.dma_start(out=rows, in_=vector)
             raw_pieces.extend([raw[:, :, c : c + PIECE] for c in range(0, width, PIECE)])
+        nc.sync.dma_start(
+            out=affine_rows[GAMMA_ROW:BETA_ROW, :], in_=gamma2.rearrange("(c p) -> c p", p=P)
+        )
+        nc.sync.dma_start(
+            out=affine_rows[BETA_ROW:AFFINE_ROWS, :], in_=beta2.rearrange("(c p) -> c p", p=P)
+        )
 
         h_words = h_sb[:].bitcast(F32).rearrange("r (p u) -> r u p", u=2)
         hT_ps = psum.tile([P, 2, TOKENS], F32)
@@ -105,7 +114,7 @@ def tile_encoderblock_pb_s_kernel(tc, h, W1, b1, W2, b2, gamma2, beta2, out):
         def stand_h_up():
             for u in range(2):
                 nc.tensor.transpose(hT_ps[:, u, :], h_words[:, u, :], ident_f32[:])
-            nc.scalar.copy(
+            nc.vector.tensor_copy(
                 out=h_grouped[:].bitcast(F32).rearrange("p (r u) -> p r u", u=2),
                 in_=hT_ps[:].rearrange("p u r -> p r u"),
             )
@@ -115,28 +124,26 @@ def tile_encoderblock_pb_s_kernel(tc, h, W1, b1, W2, b2, gamma2, beta2, out):
                 out=h_codes[:].bitcast(FP8X4), scales=h_scales[:], in_=h_grouped[:]
             )
 
-        vec_ps = psum.tile([P, P], BF16)
-        vec_cols = keep.tile([P, ROWS_END], BF16)
+        vec_ps = psum.tile([P, 2, P], BF16)
+        bias_cols = keep.tile([P, BIAS_ROWS], BF16)
+        affine_cols = keep.tile([P, AFFINE_ROWS], BF16)
         b2_ps = psum.tile([P, D_MODEL], BF16)
         affine_ps = psum.tile([P, 2, D_MODEL], BF16)
         h_plus_b2 = keep.tile([TOKENS, D_MODEL], F32)
 
-        def stand_vectors_up():
-            nc.tensor.transpose(vec_ps[:], vec_rows[:], ident_bf16[:])
+        def stand_up(i, rows):
+            nc.tensor.transpose(vec_ps[:, i, :], rows[:], ident_bf16[:])
 
-        def spread_vectors():
-            nc.scalar.copy(out=vec_cols[:], in_=vec_ps[:, 0:ROWS_END])
-            for row, spread in (
-                (B2_ROW, b2_ps[:]),
-                (GAMMA_ROW, affine_ps[:, 0, :]),
-                (BETA_ROW, affine_ps[:, 1, :]),
-            ):
-                for c in range(D_MODEL // P):
-                    nc.tensor.transpose(
-                        spread[:, c * P : (c + 1) * P],
-                        vec_cols[:, row + c : row + c + 1].to_broadcast([P, P]),
-                        ident_bf16[:],
-                    )
+        def keep_columns(i, cols):
+            nc.scalar.copy(out=cols[:], in_=vec_ps[:, i, 0 : cols.shape[1]])
+
+        def spread(out, cols, row):
+            for c in range(D_MODEL // P):
+                nc.tensor.transpose(
+                    out[:, c * P : (c + 1) * P],
+                    cols[:, row + c : row + c + 1].to_broadcast([P, P]),
+                    ident_bf16[:],
+                )
 
         def add_b2_to_h():
             nc.vector.tensor_tensor(out=h_plus_b2[:], in0=h_sb[:], in1=b2_ps[:], op=ALU.add)
@@ -174,7 +181,8 @@ def tile_encoderblock_pb_s_kernel(tc, h, W1, b1, W2, b2, gamma2, beta2, out):
         ]
 
         def regroup_piece(i):
-            regroup(nc, grouped[i][:], raw_pieces[i])
+            scalar_cols = SCALAR_COLS_FIRST if i < FIRST_PIECES else SCALAR_COLS
+            regroup(nc, grouped[i][:], raw_pieces[i], scalar_cols)
 
         def first_layer(i):
             for m in range(0, PIECE, P):
@@ -193,7 +201,7 @@ def tile_encoderblock_pb_s_kernel(tc, h, W1, b1, W2, b2, gamma2, beta2, out):
             nc.vector.tensor_tensor(
                 out=f1_grouped[g][:],
                 in0=f1_ps[g][:].rearrange("p j r -> p r j"),
-                in1=vec_cols[:, B1_ROW + g * PACK : B1_ROW + (g + 1) * PACK]
+                in1=bias_cols[:, B1_ROW + g * PACK : B1_ROW + (g + 1) * PACK]
                 .unsqueeze(1)
                 .to_broadcast([P, TOKENS, PACK]),
                 op=ALU.add,
@@ -231,10 +239,11 @@ def tile_encoderblock_pb_s_kernel(tc, h, W1, b1, W2, b2, gamma2, beta2, out):
         stand_h_up()
         quantise_piece(0)
         quantise_h()
-        stand_vectors_up()
+        stand_up(0, bias_rows)
         multiply(0)
         weights_round(1)
-        spread_vectors()
+        keep_columns(0, bias_cols)
+        spread(b2_ps[:], bias_cols, B2_ROW)
         weights_round(2)
         add_b1(0)
         weights_round(3)
@@ -245,7 +254,11 @@ def tile_encoderblock_pb_s_kernel(tc, h, W1, b1, W2, b2, gamma2, beta2, out):
         weights_round(5)
         quantise_f1(1)
         weights_round(6)
+        stand_up(1, affine_rows)
+        keep_columns(1, affine_cols)
         weights_round(7)
+        spread(affine_ps[:, 0, :], affine_cols, GAMMA_ROW)
+        spread(affine_ps[:, 1, :], affine_cols, BETA_ROW)
 
         u = keep.tile([TOKENS, D_MODEL], F32)
         stats = keep.tile([TOKENS, OUT_PIECES, 6], F32)

@@ -24,10 +24,8 @@ PASSES_2 = D_HIDDEN // K_PASS
 PIECE = 256
 W1_LOADS = (256, 256, 256, 256)
 W2_LOADS = (512,)
-RUN = 4
-FIRST_PIECES = 2
-SCALAR_COLS_FIRST = PIECE // 2
-SCALAR_COLS = PIECE * 13 // 16
+RUN = 8
+SCALAR_COLS = (96, 128, 192, 192, 208, 208, 208, 208)
 
 FLOPS = 2 * TOKENS * D_MODEL * D_HIDDEN * 2
 
@@ -181,8 +179,7 @@ def tile_encoderblock_pb_s_kernel(tc, h, W1, b1, W2, b2, gamma2, beta2, out):
         ]
 
         def regroup_piece(i):
-            scalar_cols = SCALAR_COLS_FIRST if i < FIRST_PIECES else SCALAR_COLS
-            regroup(nc, grouped[i][:], raw_pieces[i], scalar_cols)
+            regroup(nc, grouped[i][:], raw_pieces[i], SCALAR_COLS[i])
 
         def first_layer(i):
             for m in range(0, PIECE, P):
@@ -235,9 +232,9 @@ def tile_encoderblock_pb_s_kernel(tc, h, W1, b1, W2, b2, gamma2, beta2, out):
             multiply(i)
 
         regroup_piece(0)
-        regroup_piece(1)
-        stand_h_up()
         quantise_piece(0)
+        stand_h_up()
+        regroup_piece(1)
         quantise_h()
         stand_up(0, bias_rows)
         multiply(0)
@@ -248,14 +245,14 @@ def tile_encoderblock_pb_s_kernel(tc, h, W1, b1, W2, b2, gamma2, beta2, out):
         add_b1(0)
         weights_round(3)
         quantise_f1(0)
-        add_b2_to_h()
         weights_round(4)
         add_b1(1)
+        stand_up(1, affine_rows)
         weights_round(5)
         quantise_f1(1)
         weights_round(6)
-        stand_up(1, affine_rows)
         keep_columns(1, affine_cols)
+        add_b2_to_h()
         weights_round(7)
         spread(affine_ps[:, 0, :], affine_cols, GAMMA_ROW)
         spread(affine_ps[:, 1, :], affine_cols, BETA_ROW)

@@ -23,7 +23,7 @@ PASSES_2 = D_HIDDEN // K_PASS
 
 PIECE = 256
 W1_LOADS = (256, 256, 256, 256)
-W2_LOADS = (512,)
+W2_LOADS = (256, 256)
 RUN = 8
 SCALAR_COLS = (96, 128, 192, 192, 208, 208, 208, 208)
 

@@ -68,13 +68,15 @@ def tile_encoderblock_pb_s_kernel(tc, h, W1, b1, W2, b2, gamma2, beta2, out):
         make_identity(nc, ident_bf16[:])
 
         h_sb = keep.tile([TOKENS, D_MODEL], BF16)
-        nc.scalar.dma_start(out=h_sb[:], in_=h.rearrange("b s d -> (b s) d"))
         B1_ROW, B2_ROW, BIAS_ROWS = 0, 8, 12
         GAMMA_ROW, BETA_ROW, AFFINE_ROWS = 0, 4, 8
-        biases = (
-            (bias_rows[B1_ROW:B2_ROW, :], b1.rearrange("(c p) -> c p", p=P)),
-            (bias_rows[B2_ROW:BIAS_ROWS, :], b2.rearrange("(c p) -> c p", p=P)),
-        )
+        small_loads = {
+            0: ((h_sb[:], h.rearrange("b s d -> (b s) d")),),
+            1: (
+                (bias_rows[B1_ROW:B2_ROW, :], b1.rearrange("(c p) -> c p", p=P)),
+                (bias_rows[B2_ROW:BIAS_ROWS, :], b2.rearrange("(c p) -> c p", p=P)),
+            ),
+        }
 
         table_warm = keep.tile([P, 1], F32)
         nc.scalar.activation(out=table_warm[:], in_=eps[:], func=ACT.Abs_reciprocal_sqrt)
@@ -92,9 +94,8 @@ def tile_encoderblock_pb_s_kernel(tc, h, W1, b1, W2, b2, gamma2, beta2, out):
             width = source.shape[2]
             raw = keep.tile([P, PACK, width], BF16, name="raw%d" % i)
             nc.sync.dma_start(out=raw[:], in_=source)
-            if i == 0:
-                for rows, vector in biases:
-                    nc.sync.dma_start(out=rows, in_=vector)
+            for tile, small in small_loads.get(i, ()):
+                nc.sync.dma_start(out=tile, in_=small)
             raw_pieces.extend([raw[:, :, c : c + PIECE] for c in range(0, width, PIECE)])
         nc.sync.dma_start(
             out=affine_rows[GAMMA_ROW:BETA_ROW, :], in_=gamma2.rearrange("(c p) -> c p", p=P)

from contextlib import ExitStack

import concourse.mybir as mybir
from concourse.masks import make_identity

F32 = mybir.dt.float32
BF16 = mybir.dt.bfloat16
U32 = mybir.dt.uint32
U8 = mybir.dt.uint8
FP8X4 = mybir.dt.float8_e4m3fn_x4
ALU = mybir.AluOpType
ACT = mybir.ActivationFunctionType

P = 128
PACK = 4
K_PASS = P * PACK

TOKENS = 128
D_MODEL = 512
D_HIDDEN = 1024
EPS = 1e-14
PASSES_2 = D_HIDDEN // K_PASS

PIECE = 256
W1_LOADS = (256, 256, 256, 256)
W2_LOADS = (256, 256)
RUN = 8
SCALAR_COLS = (96, 128, 192, 192, 208, 208, 208, 208)

FLOPS = 2 * TOKENS * D_MODEL * D_HIDDEN * 2


def regroup(nc, grouped, raw, scalar_cols):
    for copy, cols in (
        (nc.scalar.copy, slice(0, scalar_cols)),
        (nc.vector.tensor_copy, slice(scalar_cols, PIECE)),
    ):
        copy(
            out=grouped[:, cols, :].rearrange("p (c i) j -> p c j i", i=RUN),
            in_=raw[:, :, cols].rearrange("p j (c i) -> p c j i", i=RUN),
        )


def quantise(nc, codes, scales, grouped):
    nc.vector.quantize_mx(
        out=codes.bitcast(FP8X4),
        scales=scales,
        in_=grouped.rearrange("p c j -> p (c j)"),
    )


def tile_encoderblock_pb_s_kernel(tc, h, W1, b1, W2, b2, gamma2, beta2, out):
    nc = tc.nc
    with ExitStack() as ctx:
        keep = ctx.enter_context(tc.tile_pool(name="keep", bufs=1))
        psum = ctx.enter_context(tc.psum_pool(name="psum", bufs=1))
        ctx.enter_context(tc.manual_schedule())

        bias_rows = keep.tile([P, P], BF16)
        nc.vector.memset(bias_rows[:], 0.0)
        affine_rows = keep.tile([P, P], BF16)
        nc.vector.memset(affine_rows[:], 0.0)
        eps = keep.tile([P, 1], F32)
        nc.vector.memset(eps[:], EPS)
        ident_f32 = keep.tile([P, P], F32)
        make_identity(nc, ident_f32[:])
        ident_bf16 = keep.tile([P, P], BF16)
        make_identity(nc, ident_bf16[:])

        h_sb = keep.tile([TOKENS, D_MODEL], BF16)
        B1_ROW, B2_ROW, BIAS_ROWS = 0, 8, 12
        GAMMA_ROW, BETA_ROW, AFFINE_ROWS = 0, 4, 8
        small_loads = {
            0: ((h_sb[:], h.rearrange("b s d -> (b s) d")),),
            1: (
                (bias_rows[B1_ROW:B2_ROW, :], b1.rearrange("(c p) -> c p", p=P)),
                (bias_rows[B2_ROW:BIAS_ROWS, :], b2.rearrange("(c p) -> c p", p=P)),
            ),
        }

        table_warm = keep.tile([P, 1], F32)
        nc.scalar.activation(out=table_warm[:], in_=eps[:], func=ACT.Abs_reciprocal_sqrt)

        w1_rows = W1.rearrange("(p j) f -> p j f", j=PACK)
        w2_rows = W2.rearrange("(g j p) n -> g p j n", j=PACK, p=P)
        loads = []
        for rows, widths in ((w1_rows, W1_LOADS), (w2_rows[0], W2_LOADS), (w2_rows[1], W2_LOADS)):
            start = 0
            for width in widths:
                loads.append(rows[:, :, start : start + width])
                start += width
        raw_pieces = []
        for i, source in enumerate(loads):
            width = source.shape[2]
            raw = keep.tile([P, PACK, width], BF16, name="raw%d" % i)
            nc.sync.dma_start(out=raw[:], in_=source)
            for tile, small in small_loads.get(i, ()):
                nc.sync.dma_start(out=tile, in_=small)
            raw_pieces.extend([raw[:, :, c : c + PIECE] for c in range(0, width, PIECE)])
        nc.sync.dma_start(
            out=affine_rows[GAMMA_ROW:BETA_ROW, :], in_=gamma2.rearrange("(c p) -> c p", p=P)
        )
        nc.sync.dma_start(
            out=affine_rows[BETA_ROW:AFFINE_ROWS, :], in_=beta2.rearrange("(c p) -> c p", p=P)
        )

        h_words = h_sb[:].bitcast(F32).rearrange("r (p u) -> r u p", u=2)
        hT_ps = psum.tile([P, 2, TOKENS], F32)
        h_grouped = keep.tile([P, TOKENS * PACK], BF16, align_bytes=64)
        h_codes = keep.tile([P, TOKENS], U32, align_bytes=64)
        h_scales = keep.tile([P, TOKENS], U8, align_bytes=64)

        def stand_h_up():
            for u in range(2):
                nc.tensor.transpose(hT_ps[:, u, :], h_words[:, u, :], ident_f32[:])
            nc.vector.tensor_copy(
                out=h_grouped[:].bitcast(F32).rearrange("p (r u) -> p r u", u=2),
                in_=hT_ps[:].rearrange("p u r -> p r u"),
            )

        def quantise_h():
            nc.vector.quantize_mx(
                out=h_codes[:].bitcast(FP8X4), scales=h_scales[:], in_=h_grouped[:]
            )

        vec_ps = psum.tile([P, 2, P], BF16)
        bias_cols = keep.tile([P, BIAS_ROWS], BF16)
        affine_cols = keep.tile([P, AFFINE_ROWS], BF16)
        b2_ps = psum.tile([P, D_MODEL], BF16)
        affine_ps = psum.tile([P, 2, D_MODEL], BF16)
        h_plus_b2 = keep.tile([TOKENS, D_MODEL], F32)

        def stand_up(i, rows):
            nc.tensor.transpose(vec_ps[:, i, :], rows[:], ident_bf16[:])

        def keep_columns(i, cols):
            nc.scalar.copy(out=cols[:], in_=vec_ps[:, i, 0 : cols.shape[1]])

        def spread(out, cols, row):
            for c in range(D_MODEL // P):
                nc.tensor.transpose(
                    out[:, c * P : (c + 1) * P],
                    cols[:, row + c : row + c + 1].to_broadcast([P, P]),
                    ident_bf16[:],
                )

        def add_b2_to_h():
            nc.vector.tensor_tensor(out=h_plus_b2[:], in0=h_sb[:], in1=b2_ps[:], op=ALU.add)

        N_PIECES = len(raw_pieces)
        W1_PIECES = D_HIDDEN // PIECE
        OUT_PIECES = D_MODEL // PIECE
        grouped = [
            keep.tile([P, PIECE, PACK], BF16, align_bytes=64, name="grouped%d" % i)
            for i in range(N_PIECES)
        ]
        codes = [
            keep.tile([P, PIECE], U32, align_bytes=64, name="codes%d" % i)
            for i in range(N_PIECES)
        ]
        scales = [
            keep.tile([P, PIECE], U8, align_bytes=64, name="scales%d" % i)
            for i in range(N_PIECES)
        ]
        f1_grouped = [
            keep.tile([P, TOKENS, PACK], BF16, align_bytes=64, name="f1_grouped%d" % g)
            for g in range(PASSES_2)
        ]
        f1_codes = [
            keep.tile([P, TOKENS], U32, align_bytes=64, name="f1_codes%d" % g)
            for g in range(PASSES_2)
        ]
        f1_scales = [
            keep.tile([P, TOKENS], U8, align_bytes=64, name="f1_scales%d" % g)
            for g in range(PASSES_2)
        ]
        f1_ps = [psum.tile([P, PACK, TOKENS], F32, name="f1_ps%d" % g) for g in range(PASSES_2)]
        f2_ps = [
            psum.tile([TOKENS, PIECE], F32, name="f2_ps%d" % n) for n in range(OUT_PIECES)
        ]

        def regroup_piece(i):
            regroup(nc, grouped[i][:], raw_pieces[i], SCALAR_COLS[i])

        def first_layer(i):
            for m in range(0, PIECE, P):
                g, j = divmod((i * PIECE + m) // P, PACK)
                nc.tensor.matmul_mx(
                    out=f1_ps[g][:, j, :],
                    lhsT=codes[i][:, m : m + P].bitcast(FP8X4),
                    lhsT_scale=scales[i][:, m : m + P],
                    rhs=h_codes[:].bitcast(FP8X4),
                    rhs_scale=h_scales[:],
                    start=True,
                    stop=True,
                )

        def add_b1(g):
            nc.vector.tensor_tensor(
                out=f1_grouped[g][:],
                in0=f1_ps[g][:].rearrange("p j r -> p r j"),
                in1=bias_cols[:, B1_ROW + g * PACK : B1_ROW + (g + 1) * PACK]
                .unsqueeze(1)
                .to_broadcast([P, TOKENS, PACK]),
                op=ALU.add,
            )

        def second_layer(i):
            g, n = divmod(i - W1_PIECES, OUT_PIECES)
            nc.tensor.matmul_mx(
                out=f2_ps[n][:],
                lhsT=f1_codes[g][:].bitcast(FP8X4),
                lhsT_scale=f1_scales[g][:],
                rhs=codes[i][:].bitcast(FP8X4),
                rhs_scale=scales[i][:],
                start=(g == 0),
                stop=(g == PASSES_2 - 1),
            )

        def quantise_f1(g):
            quantise(nc, f1_codes[g][:], f1_scales[g][:], f1_grouped[g][:])

        def quantise_piece(i):
            quantise(nc, codes[i][:], scales[i][:], grouped[i][:])

        def multiply(i):
            (first_layer if i < W1_PIECES else second_layer)(i)

        def weights_round(i):
            if i + 1 < N_PIECES:
                regroup_piece(i + 1)
            quantise_piece(i)
            multiply(i)

        regroup_piece(0)
        quantise_piece(0)
        stand_h_up()
        regroup_piece(1)
        quantise_h()
        stand_up(0, bias_rows)
        multiply(0)
        weights_round(1)
        keep_columns(0, bias_cols)
        spread(b2_ps[:], bias_cols, B2_ROW)
        weights_round(2)
        add_b1(0)
        weights_round(3)
        quantise_f1(0)
        weights_round(4)
        add_b1(1)
        stand_up(1, affine_rows)
        weights_round(5)
        quantise_f1(1)
        weights_round(6)
        keep_columns(1, affine_cols)
        add_b2_to_h()
        weights_round(7)
        spread(affine_ps[:, 0, :], affine_cols, GAMMA_ROW)
        spread(affine_ps[:, 1, :], affine_cols, BETA_ROW)

        u = keep.tile([TOKENS, D_MODEL], F32)
        stats = keep.tile([TOKENS, OUT_PIECES, 6], F32)
        for n in range(OUT_PIECES):
            cols = slice(n * PIECE, (n + 1) * PIECE)
            nc.vector.tensor_tensor(
                out=u[:, cols], in0=f2_ps[n][:], in1=h_plus_b2[:, cols], op=ALU.add
            )
        for n in range(OUT_PIECES):
            cols = slice(n * PIECE, (n + 1) * PIECE)
            nc.vector.bn_stats(out=stats[:, n, :], in_=u[:, cols])
        mean_var = keep.tile([TOKENS, 2], F32)
        nc.vector.bn_aggr(out=mean_var[:], in_=stats[:].rearrange("p n s -> p (n s)"))
        rstd = keep.tile([TOKENS, 1], F32)
        nc.scalar.activation(
            out=rstd[:], in_=mean_var[:, 1:2], func=ACT.Abs_reciprocal_sqrt, bias=eps[:]
        )
        centred = keep.tile([TOKENS, D_MODEL], F32)
        halves = [slice(n * PIECE, (n + 1) * PIECE) for n in range(OUT_PIECES)]
        for cols in halves:
            nc.vector.scalar_tensor_tensor(
                out=centred[:, cols],
                in0=u[:, cols],
                scalar=mean_var[:, 0:1],
                in1=affine_ps[:, 0, cols],
                op0=ALU.subtract,
                op1=ALU.mult,
            )
        result = keep.tile([TOKENS, D_MODEL], F32)
        out_rows = out.rearrange("b s d -> (b s) d")
        for cols in halves:
            nc.vector.scalar_tensor_tensor(
                out=result[:, cols],
                in0=centred[:, cols],
                scalar=rstd[:],
                in1=affine_ps[:, 1, cols],
                op0=ALU.mult,
                op1=ALU.add,
            )
            nc.sync.dma_start(out=out_rows[:, cols], in_=result[:, cols])
